import numpy as np
import ml_dtypes


def mxq(x, axis, fmt="e4m3"):
    dtype, down = {"e4m3": (ml_dtypes.float8_e4m3fn, 7), "e5m2": (ml_dtypes.float8_e5m2, 14)}[fmt]
    v = np.moveaxis(np.asarray(x, np.float32).astype(ml_dtypes.bfloat16).astype(np.float64), axis, -1)
    blocks = v.reshape(v.shape[:-1] + (-1, 32))
    amax = np.abs(blocks).max(-1, keepdims=True)
    byte = np.maximum(np.where(amax > 0, np.frexp(amax)[1] - 1 + 127, 0) - down, 1)
    scale = np.exp2(byte - 127.0)
    codes = (blocks / scale).astype(np.float32).astype(dtype).astype(np.float64)
    return np.moveaxis((codes * scale).reshape(v.shape), -1, axis)


WIDE = False


def mx_kscale(k):
    if not WIDE:
        return np.ones(k)
    levels = np.array([10, -10, 5, -5, 0])
    a = np.random.permutation(np.resize(levels, k // 512 * 4)).reshape(k // 512, 4)
    idx = np.arange(k)
    return np.exp2(a[idx // 512, idx % 128 // 32])


BF16 = ml_dtypes.bfloat16


def bf(x):
    return np.asarray(x, np.float32).astype(BF16)


def f64(x):
    return np.asarray(x).astype(np.float64)


E2M1 = np.array([0.0, 0.5, 1.0, 1.5, 2.0, 3.0, 4.0, 6.0, -0.0, -0.5, -1.0, -1.5, -2.0, -3.0, -4.0, -6.0])


def pack_weight(w, fmt):
    k, n = w.shape
    w = f64(bf(w)).reshape(k // 32, 32, n)
    amax = np.abs(w).max(1)
    if fmt == "e4m3":
        byte = np.frexp(amax)[1] - 1 + 127 - 7
    else:
        mant, ex = np.frexp(amax / 6.0)
        byte = np.where(mant > 0.5, ex, ex - 1) + 127
    byte = np.clip(np.where(amax > 0, byte, 1), 1, 254)
    scaled = (w * np.exp2(127.0 - byte)[:, None, :]).reshape(k, n).astype(np.float32)
    by_word = np.ascontiguousarray(scaled.reshape(k // 512, 128, 4, n).transpose(0, 1, 3, 2))
    if fmt == "e4m3":
        words = by_word.astype(ml_dtypes.float8_e4m3fn).view(np.uint8)
    else:
        c = by_word.astype(ml_dtypes.float4_e2m1fn).view(np.uint8) & 0xF
        words = c[..., 0::2] | (c[..., 1::2] << 4)
    return np.ascontiguousarray(words), np.ascontiguousarray(byte.astype(np.uint8).reshape(k // 512, 16, n))


def unpack_weight(words, scales, fmt):
    g, p, n, _ = words.shape
    if fmt == "e4m3":
        vals = np.ascontiguousarray(words).view(ml_dtypes.float8_e4m3fn).astype(np.float64)
    else:
        nib = np.empty((g, p, n, 4), np.uint8)
        nib[..., 0::2] = words & 0xF
        nib[..., 1::2] = words >> 4
        vals = E2M1[nib]
    vals = vals * np.repeat(np.exp2(scales.astype(np.float64) - 127.0), 8, axis=1)[..., None]
    return vals.transpose(0, 1, 3, 2).reshape(g * 512, n)


B, T, STOCH, ACT, HID, DETER, G = 4, 64, 1024, 512, 512, 4096, 8
N = B * T
BH = DETER // G
BLK_IN = BH + 3 * HID
EPS = 1e-3
FMT = "e4m3"


def silu(v):
    return v / (1.0 + np.exp(-v))


def ln(v, g, b):
    mu = v.mean(-1, keepdims=True)
    var = v.var(-1, keepdims=True)
    return (v - mu) / np.sqrt(var + EPS) * g + b


def setup_inputs():
    ss, sa, sd = mx_kscale(STOCH), mx_kscale(ACT), mx_kscale(DETER)
    w_hid = np.random.standard_normal((G, BLK_IN, BH)) * 0.2 / np.sqrt(BLK_IN)
    w_hid[:, :BH] = w_hid[:, :BH] / sd.reshape(G, BH)[:, :, None]
    s = bf(np.random.standard_normal((B, T, STOCH)) * ss)
    a = bf(np.random.standard_normal((B, T, ACT)) * sa)
    d = bf(np.random.standard_normal((B, T, DETER)) * sd)
    W_s_words, W_s_scales = pack_weight(np.random.standard_normal((STOCH, HID)) * 0.15 / np.sqrt(STOCH) / ss[:, None], FMT)
    W_a_words, W_a_scales = pack_weight(np.random.standard_normal((ACT, HID)) * 0.15 / np.sqrt(ACT) / sa[:, None], FMT)
    W_d_words, W_d_scales = pack_weight(np.random.standard_normal((DETER, HID)) * 0.15 / np.sqrt(DETER) / sd[:, None], FMT)
    return {
        "s": s,
        "a": a,
        "d": d,
        "W_s_words": W_s_words,
        "W_s_scales": W_s_scales,
        "W_a_words": W_a_words,
        "W_a_scales": W_a_scales,
        "W_d_words": W_d_words,
        "W_d_scales": W_d_scales,
        "ln_s_g": bf(1.0 + 0.1 * np.random.standard_normal(HID)),
        "ln_s_b": bf(0.2 * np.random.standard_normal(HID)),
        "ln_a_g": bf(1.0 + 0.1 * np.random.standard_normal(HID)),
        "ln_a_b": bf(0.2 * np.random.standard_normal(HID)),
        "ln_d_g": bf(1.0 + 0.1 * np.random.standard_normal(HID)),
        "ln_d_b": bf(0.2 * np.random.standard_normal(HID)),
        "W_hid": bf(w_hid),
        "ln_h_g": bf(1.0 + 0.1 * np.random.standard_normal(DETER)),
        "ln_h_b": bf(0.2 * np.random.standard_normal(DETER)),
    }


def reference(s, a, d, W_s_words, W_s_scales, W_a_words, W_a_scales, W_d_words, W_d_scales, ln_s_g, ln_s_b, ln_a_g, ln_a_b, ln_d_g, ln_d_b, W_hid, ln_h_g, ln_h_b):
    sq = mxq(f64(s).reshape(N, STOCH), 1, "e4m3")
    aq = mxq(f64(a).reshape(N, ACT), 1, "e4m3")
    dq = mxq(f64(d).reshape(N, DETER), 1, "e4m3")
    s_h = silu(ln(sq @ unpack_weight(W_s_words, W_s_scales, FMT), f64(ln_s_g), f64(ln_s_b)))
    a_h = silu(ln(aq @ unpack_weight(W_a_words, W_a_scales, FMT), f64(ln_a_g), f64(ln_a_b)))
    d_h = silu(ln(dq @ unpack_weight(W_d_words, W_d_scales, FMT), f64(ln_d_g), f64(ln_d_b)))
    xq = mxq(np.concatenate([s_h, a_h, d_h], axis=-1), 1, "e4m3")
    wq = mxq(f64(W_hid), 1, "e4m3")
    p = (dq.reshape(N, G, BH).transpose(1, 0, 2) @ wq[:, :BH]) + (xq @ wq[:, BH:])
    p = p.transpose(1, 0, 2).reshape(N, DETER)
    return silu(ln(p, f64(ln_h_g), f64(ln_h_b)))

@@ -1,0 +1,318 @@
+from contextlib import ExitStack
+
+import concourse.mybir as mybir
+from concourse.masks import make_identity
+
+FP8X4 = mybir.dt.float8_e4m3fn_x4
+BF16 = mybir.dt.bfloat16
+F32 = mybir.dt.float32
+I32 = mybir.dt.int32
+U32 = mybir.dt.uint32
+U8 = mybir.dt.uint8
+ALU = mybir.AluOpType
+ACT = mybir.ActivationFunctionType
+
+P = 128
+PACK = 4
+K_PASS = P * PACK
+ROWS = 256
+ROW_TILES = ROWS // P
+HID = 512
+BLOCKS = 8
+DETER = BLOCKS * HID
+STREAM_PASSES = (2, 1, 8)
+FIRST_PASS = (0, 2, 3)
+ALL_PASSES = 11
+D_STREAM = 2
+BLOCK_PASSES = 4
+EPS = 1e-3
+LOAD_COLS = 1024
+VECTOR_COLS = 192
+
+FLOPS = 2 * ROWS * ((1024 + 512 + 4096) * HID + BLOCK_PASSES * K_PASS * DETER)
+
+
+def tile_blockrecurrentmodel_pa_kernel(
+    tc,
+    s,
+    a,
+    d,
+    W_s_words,
+    W_s_scales,
+    W_a_words,
+    W_a_scales,
+    W_d_words,
+    W_d_scales,
+    ln_s_g,
+    ln_s_b,
+    ln_a_g,
+    ln_a_b,
+    ln_d_g,
+    ln_d_b,
+    W_hid,
+    ln_h_g,
+    ln_h_b,
+    out,
+):
+    nc = tc.nc
+    stream_rows = (s.flatten_outer_dims(), a.flatten_outer_dims(), d.flatten_outer_dims())
+    stream_words = (W_s_words, W_a_words, W_d_words)
+    stream_scales = (W_s_scales, W_a_scales, W_d_scales)
+    stream_gains = (ln_s_g, ln_a_g, ln_d_g)
+    stream_biases = (ln_s_b, ln_a_b, ln_d_b)
+
+    with ExitStack() as pools:
+        keep = pools.enter_context(tc.tile_pool(name="keep", bufs=1))
+        small = pools.enter_context(tc.tile_pool(name="small", bufs=4))
+        stage = pools.enter_context(tc.tile_pool(name="stage", bufs=2))
+        normed = pools.enter_context(tc.tile_pool(name="normed", bufs=4))
+        w_raw_pool = pools.enter_context(tc.tile_pool(name="w_raw", bufs=8))
+        w_grouped_pool = pools.enter_context(tc.tile_pool(name="w_grouped", bufs=6))
+        w_packed_pool = pools.enter_context(tc.tile_pool(name="w_packed", bufs=12))
+        psum_t = pools.enter_context(tc.psum_pool(name="psum_t", bufs=2))
+        psum_acc = pools.enter_context(tc.psum_pool(name="psum_acc", bufs=6))
+
+        ident = keep.tile([P, P], F32)
+        make_identity(nc, ident[:])
+        ident_bf = keep.tile([P, P], BF16)
+        make_identity(nc, ident_bf[:])
+        neg_half = keep.tile([P, ROW_TILES], F32)
+        nc.vector.memset(neg_half[:], -0.5)
+
+        w_words = keep.tile([P, ALL_PASSES, HID * PACK], U8, align_bytes=64)
+        w_planes = keep.tile([P, ALL_PASSES, HID], U8, align_bytes=64)
+        nc.vector.memset(w_planes[:].rearrange("p c n -> p (c n)").bitcast(I32), 0)
+        act_codes = keep.tile([P, ALL_PASSES, ROWS], U32, align_bytes=64)
+        act_scales = keep.tile([P, ALL_PASSES, ROWS], U8, align_bytes=64)
+        x_codes = keep.tile([P, 3, ROWS], U32, align_bytes=64)
+        x_scales = keep.tile([P, 3, ROWS], U8, align_bytes=64)
+        scaled = keep.tile([P, ROW_TILES, DETER], F32)
+        h_stats = keep.tile([P, ROW_TILES, BLOCKS, 6], F32)
+
+        w_raw = []
+
+        def load_w_piece():
+            g, c = divmod(len(w_raw), BLOCK_PASSES)
+            raw = w_raw_pool.tile([P, PACK, HID], BF16)
+            nc.sync.dma_start(
+                out=raw[:], in_=W_hid[g, c * K_PASS : (c + 1) * K_PASS, :].rearrange("(p j) n -> p j n", j=PACK)
+            )
+            w_raw.append(raw)
+
+        rows_sb = [None, None, None]
+        for c in (2, 0, 1):
+            passes = STREAM_PASSES[c]
+            first = FIRST_PASS[c]
+            rows_c = keep.tile([P, ROW_TILES, passes * K_PASS], BF16, name="rows_%d" % c)
+            rows_sb[c] = rows_c
+            for k0 in range(0, passes * K_PASS, LOAD_COLS):
+                k1 = min(k0 + LOAD_COLS, passes * K_PASS)
+                nc.sync.dma_start(
+                    out=rows_c[:, :, k0:k1], in_=stream_rows[c].rearrange("(m p) k -> p m k", p=P)[:, :, k0:k1]
+                )
+            for r in range(4):
+                nc.sync.dma_start(
+                    out=w_planes[r:P:32, first : first + passes, :].bitcast(I32),
+                    in_=stream_scales[c].rearrange("g (q r) n -> r q g n", r=4)[r].bitcast(I32),
+                )
+            for g0 in range(0, passes, 4):
+                g1 = min(g0 + 4, passes)
+                nc.sync.dma_start(
+                    out=w_words[:, first + g0 : first + g1, :].bitcast(I32),
+                    in_=stream_words[c][g0:g1].rearrange("g p n t -> p g (n t)").bitcast(I32),
+                )
+            for i in range(2):
+                load_w_piece()
+
+        gb_raw = keep.tile([P, 6, 16], BF16)
+        for c in range(3):
+            nc.sync.dma_start(out=gb_raw[:, c, :PACK], in_=stream_gains[c].rearrange("(p t) -> p t", t=PACK))
+            nc.sync.dma_start(out=gb_raw[:, 3 + c, :PACK], in_=stream_biases[c].rearrange("(p t) -> p t", t=PACK))
+        gb_cols = keep.tile([P, 6, PACK], F32)
+        nc.vector.tensor_copy(out=gb_cols[:], in_=gb_raw[:, :, :PACK])
+
+        gain_bc = keep.tile([P, DETER], BF16)
+        nc.sync.dma_start(out=gain_bc[:], in_=ln_h_g.partition_broadcast(P))
+
+        gain_bias_rows = keep.tile([P, DETER], BF16)
+        nc.gpsimd.memset(gain_bias_rows[:].bitcast(F32), 0.0)
+        nc.sync.dma_start(out=gain_bias_rows[0:4, :], in_=ln_h_g.partition_broadcast(4))
+        nc.sync.dma_start(out=gain_bias_rows[4:5, :], in_=ln_h_b.partition_broadcast(1))
+        shift_cols = keep.tile([P, ROW_TILES, P], BF16)
+        nc.vector.memset(shift_cols[:], 0.0)
+        nc.vector.memset(shift_cols[:, :, 4:5], 1.0)
+
+        def norm_factors(mean_var):
+            var_eps = small.tile([P, ROW_TILES], F32)
+            nc.vector.tensor_scalar(out=var_eps[:], in0=mean_var[:, :, 1], scalar1=EPS, scalar2=None, op0=ALU.add)
+            rstd = small.tile([P, ROW_TILES], F32)
+            nc.gpsimd.tensor_tensor(out=rstd[:], in0=var_eps[:], in1=neg_half[:], op=ALU.pow)
+            shift = small.tile([P, ROW_TILES], F32)
+            nc.vector.scalar_tensor_tensor(
+                out=shift[:], in0=mean_var[:, :, 0], scalar=-1.0, in1=rstd[:], op0=ALU.mult, op1=ALU.mult
+            )
+            return rstd, shift
+
+        for c in (2, 0, 1):
+            passes = STREAM_PASSES[c]
+            first = FIRST_PASS[c]
+
+            for pair in range(0, passes, 2):
+                count = min(2, passes - pair)
+                grouped = stage.tile([P, 2, ROWS, PACK], BF16, align_bytes=64)
+                for i in range(count):
+                    g = pair + i
+                    flipped = psum_t.tile([P, 2, ROWS], F32, tag="flipped")
+                    for u in range(2):
+                        for mt in range(ROW_TILES):
+                            nc.tensor.transpose(
+                                flipped[:, u, mt * P : (mt + 1) * P],
+                                rows_sb[c][:, mt, :].bitcast(F32)[:, 256 * g + u : 256 * (g + 1) : 2],
+                                ident[:],
+                            )
+                    copy_out = nc.vector.tensor_copy if i == 0 else nc.scalar.copy
+                    copy_out(out=grouped[:, i].bitcast(F32), in_=flipped[:].rearrange("p u r -> p r u"))
+                where = slice(first + pair, first + pair + count)
+                nc.vector.quantize_mx(
+                    out=act_codes[:, where, :].rearrange("p c r -> p (c r)").bitcast(FP8X4),
+                    scales=act_scales[:, where, :].rearrange("p c r -> p (c r)"),
+                    in_=grouped[:, :count].rearrange("p c r t -> p (c r t)"),
+                )
+
+            stats = small.tile([P, ROW_TILES, 6], F32)
+            mean_var = small.tile([P, ROW_TILES, 2], F32)
+            y = []
+            for mt in range(ROW_TILES):
+                y_mt = psum_acc.tile([P, HID], F32, tag="acc")
+                y.append(y_mt)
+                for i in range(passes):
+                    nc.tensor.matmul_mx(
+                        out=y_mt[:],
+                        lhsT=act_codes[:, first + i, mt * P : (mt + 1) * P].bitcast(FP8X4),
+                        lhsT_scale=act_scales[:, first + i, mt * P : (mt + 1) * P],
+                        rhs=w_words[:, first + i, :].bitcast(FP8X4),
+                        rhs_scale=w_planes[:, first + i, :],
+                        start=(i == 0),
+                        stop=(i == passes - 1),
+                    )
+                nc.vector.bn_stats(out=stats[:, mt, :], in_=y_mt[:])
+                nc.vector.bn_aggr(out=mean_var[:, mt, :], in_=stats[:, mt, :])
+            rstd, shift = norm_factors(mean_var)
+
+            z = []
+            for mt in range(ROW_TILES):
+                z_mt = normed.tile([P, PACK, P], F32, tag="z")
+                z.append(z_mt)
+                nc.scalar.activation(
+                    out=z_mt[:],
+                    in_=y[mt][:].rearrange("p (m t) -> p t m", t=PACK),
+                    func=ACT.Identity,
+                    scale=rstd[:, mt : mt + 1],
+                    bias=shift[:, mt : mt + 1],
+                )
+            x_planes = stage.tile([P, PACK, ROWS], BF16)
+            for half in range(2):
+                flipped = psum_t.tile([P, 2, ROWS], F32, tag="flipped")
+                for u in range(2):
+                    for mt in range(ROW_TILES):
+                        nc.tensor.transpose(flipped[:, u, mt * P : (mt + 1) * P], z[mt][:, 2 * half + u, :], ident[:])
+                for u in range(2):
+                    t = 2 * half + u
+                    nc.scalar.activation(
+                        out=x_planes[:, t, :],
+                        in_=flipped[:, u, :],
+                        func=ACT.Silu,
+                        scale=gb_cols[:, c, t : t + 1],
+                        bias=gb_cols[:, 3 + c, t : t + 1],
+                    )
+            x_grouped = stage.tile([P, ROWS, PACK], BF16, align_bytes=64)
+            nc.vector.tensor_copy(out=x_grouped[:], in_=x_planes[:].rearrange("p t r -> p r t"))
+            nc.vector.quantize_mx(
+                out=x_codes[:, c, :].bitcast(FP8X4),
+                scales=x_scales[:, c, :],
+                in_=x_grouped[:].rearrange("p r t -> p (r t)"),
+            )
+
+        for g in range(BLOCKS):
+            w_codes = []
+            w_scales = []
+            for c in range(BLOCK_PASSES):
+                if len(w_raw) == g * BLOCK_PASSES + c:
+                    load_w_piece()
+                raw = w_raw[g * BLOCK_PASSES + c]
+                w_grouped = w_grouped_pool.tile([P, HID, PACK], BF16, align_bytes=64)
+                nc.vector.tensor_copy(
+                    out=w_grouped[:, :VECTOR_COLS, :].rearrange("p (n i) j -> p n j i", i=4),
+                    in_=raw[:, :, :VECTOR_COLS].rearrange("p j (n i) -> p n j i", i=4),
+                )
+                nc.scalar.copy(
+                    out=w_grouped[:, VECTOR_COLS:, :].rearrange("p (n i) j -> p n j i", i=4),
+                    in_=raw[:, :, VECTOR_COLS:].rearrange("p j (n i) -> p n j i", i=4),
+                )
+                codes = w_packed_pool.tile([P, HID], U32, align_bytes=64)
+                scales = w_packed_pool.tile([P, HID], U8, align_bytes=64)
+                nc.vector.quantize_mx(
+                    out=codes[:].bitcast(FP8X4), scales=scales[:], in_=w_grouped[:].rearrange("p n j -> p (n j)")
+                )
+                w_codes.append(codes)
+                w_scales.append(scales)
+
+            cols = slice(g * HID, (g + 1) * HID)
+            for mt in range(ROW_TILES):
+                rows = slice(mt * P, (mt + 1) * P)
+                acc = psum_acc.tile([P, HID], F32, tag="acc")
+                for c in range(BLOCK_PASSES):
+                    if c == 0:
+                        lhs_codes = act_codes[:, FIRST_PASS[D_STREAM] + g, rows]
+                        lhs_scales = act_scales[:, FIRST_PASS[D_STREAM] + g, rows]
+                    else:
+                        lhs_codes = x_codes[:, c - 1, rows]
+                        lhs_scales = x_scales[:, c - 1, rows]
+                    nc.tensor.matmul_mx(
+                        out=acc[:],
+                        lhsT=lhs_codes.bitcast(FP8X4),
+                        lhsT_scale=lhs_scales,
+                        rhs=w_codes[c][:].bitcast(FP8X4),
+                        rhs_scale=w_scales[c][:],
+                        start=(c == 0),
+                        stop=(c == BLOCK_PASSES - 1),
+                    )
+                nc.vector.bn_stats(out=h_stats[:, mt, g, :], in_=acc[:])
+                nc.vector.tensor_tensor(out=scaled[:, mt, cols], in0=acc[:], in1=gain_bc[:, cols], op=ALU.mult)
+
+        h_mean_var = small.tile([P, ROW_TILES, 2], F32)
+        for mt in range(ROW_TILES):
+            nc.vector.bn_aggr(out=h_mean_var[:, mt, :], in_=h_stats[:, mt].rearrange("p g s -> p (g s)"))
+        h_rstd, h_shift = norm_factors(h_mean_var)
+
+        rest = h_shift
+        for part in range(3):
+            nc.vector.tensor_copy(out=shift_cols[:, :, part], in_=rest[:])
+            if part < 2:
+                smaller = small.tile([P, ROW_TILES], F32, tag="rest")
+                nc.vector.tensor_tensor(out=smaller[:], in0=rest[:], in1=shift_cols[:, :, part], op=ALU.subtract)
+                rest = smaller
+        shift_flipped = psum_t.tile([P, ROW_TILES, P], BF16, tag="flipped")
+        for mt in range(ROW_TILES):
+            nc.tensor.transpose(shift_flipped[:, mt, :], shift_cols[:, mt, :], ident_bf[:])
+        shift_rows = keep.tile([P, ROW_TILES, P], BF16)
+        nc.scalar.copy(out=shift_rows[:], in_=shift_flipped[:])
+
+        for mt in range(ROW_TILES):
+            for g in range(BLOCKS):
+                cols = slice(g * HID, (g + 1) * HID)
+                offset = psum_acc.tile([P, HID], F32, tag="acc")
+                nc.tensor.matmul(
+                    out=offset[:], lhsT=shift_rows[:, mt, :], rhs=gain_bias_rows[:, cols], start=True, stop=True
+                )
+                v = scaled[:, mt, cols]
+                nc.vector.scalar_tensor_tensor(
+                    out=v,
+                    in0=v,
+                    scalar=h_rstd[:, mt : mt + 1],
+                    in1=offset[:],
+                    op0=ALU.mult,
+                    op1=ALU.add,
+                )
+                nc.scalar.activation(out=v, in_=v, func=ACT.Silu)
+                nc.sync.dma_start(out=out[mt * P : (mt + 1) * P, cols], in_=v)

@@ -20,14 +20,17 @@ ROW_TILES = ROWS // P
 HID = 512
 BLOCKS = 8
 DETER = BLOCKS * HID
+S_STREAM, A_STREAM, D_STREAM = 0, 1, 2
 STREAM_PASSES = (2, 1, 8)
 FIRST_PASS = (0, 2, 3)
 ALL_PASSES = 11
-D_STREAM = 2
 BLOCK_PASSES = 4
+PIECES = BLOCKS * BLOCK_PASSES
 EPS = 1e-3
 LOAD_COLS = 1024
-VECTOR_COLS = 192
+RAW_BUFS = 7
+PACKED_BUFS = 12
+QUANTISE_LAG = 2
 
 FLOPS = 2 * ROWS * ((1024 + 512 + 4096) * HID + BLOCK_PASSES * K_PASS * DETER)
 
@@ -65,12 +68,11 @@ def tile_blockrecurrentmodel_pa_kernel(
         keep = pools.enter_context(tc.tile_pool(name="keep", bufs=1))
         small = pools.enter_context(tc.tile_pool(name="small", bufs=4))
         stage = pools.enter_context(tc.tile_pool(name="stage", bufs=2))
-        normed = pools.enter_context(tc.tile_pool(name="normed", bufs=4))
-        w_raw_pool = pools.enter_context(tc.tile_pool(name="w_raw", bufs=8))
-        w_grouped_pool = pools.enter_context(tc.tile_pool(name="w_grouped", bufs=6))
-        w_packed_pool = pools.enter_context(tc.tile_pool(name="w_packed", bufs=12))
-        psum_t = pools.enter_context(tc.psum_pool(name="psum_t", bufs=2))
-        psum_acc = pools.enter_context(tc.psum_pool(name="psum_acc", bufs=6))
+        normed = pools.enter_context(tc.tile_pool(name="normed", bufs=6))
+        w_raw_pool = pools.enter_context(tc.tile_pool(name="w_raw", bufs=RAW_BUFS))
+        w_grouped_pool = pools.enter_context(tc.tile_pool(name="w_grouped", bufs=3))
+        w_packed_pool = pools.enter_context(tc.tile_pool(name="w_packed", bufs=PACKED_BUFS))
+        psum = pools.enter_context(tc.psum_pool(name="psum", bufs=8))
 
         ident = keep.tile([P, P], F32)
         make_identity(nc, ident[:])
@@ -90,6 +92,9 @@ def tile_blockrecurrentmodel_pa_kernel(
         h_stats = keep.tile([P, ROW_TILES, BLOCKS, 6], F32)
 
         w_raw = []
+        w_grouped = []
+        w_codes = []
+        w_scales = []
 
         def load_w_piece():
             g, c = divmod(len(w_raw), BLOCK_PASSES)
@@ -99,17 +104,50 @@ def tile_blockrecurrentmodel_pa_kernel(
             )
             w_raw.append(raw)
 
-        rows_sb = [None, None, None]
-        for c in (2, 0, 1):
-            passes = STREAM_PASSES[c]
-            first = FIRST_PASS[c]
-            rows_c = keep.tile([P, ROW_TILES, passes * K_PASS], BF16, name="rows_%d" % c)
-            rows_sb[c] = rows_c
-            for k0 in range(0, passes * K_PASS, LOAD_COLS):
-                k1 = min(k0 + LOAD_COLS, passes * K_PASS)
+        def regroup_w_piece():
+            i = len(w_grouped)
+            by_vector = i % 8 in (0, 3, 6)
+            grouped = w_grouped_pool.tile(
+                [P, HID, PACK], BF16, align_bytes=64, tag="by_vector" if by_vector else "by_scalar"
+            )
+            regroup = nc.vector.tensor_copy if by_vector else nc.scalar.copy
+            regroup(
+                out=grouped[:].rearrange("p (n i) j -> p n j i", i=4),
+                in_=w_raw[i][:].rearrange("p j (n i) -> p n j i", i=4),
+            )
+            w_grouped.append(grouped)
+            if len(w_raw) < PIECES:
+                load_w_piece()
+
+        def quantise_w_piece():
+            i = len(w_codes)
+            codes = w_packed_pool.tile([P, HID], U32, align_bytes=64)
+            scales = w_packed_pool.tile([P, HID], U8, align_bytes=64)
+            nc.vector.quantize_mx(
+                out=codes[:].bitcast(FP8X4), scales=scales[:], in_=w_grouped[i][:].rearrange("p n j -> p (n j)")
+            )
+            w_codes.append(codes)
+            w_scales.append(scales)
+
+        def advance_w():
+            if len(w_grouped) < PIECES:
+                regroup_w_piece()
+            if len(w_grouped) - len(w_codes) > QUANTISE_LAG or len(w_grouped) == PIECES:
+                quantise_w_piece()
+
+        def load_rows(c):
+            width = STREAM_PASSES[c] * K_PASS
+            rows_c = keep.tile([P, ROW_TILES, width], BF16, name="rows_%d" % c)
+            for k0 in range(0, width, LOAD_COLS):
+                k1 = min(k0 + LOAD_COLS, width)
                 nc.sync.dma_start(
                     out=rows_c[:, :, k0:k1], in_=stream_rows[c].rearrange("(m p) k -> p m k", p=P)[:, :, k0:k1]
                 )
+            return rows_c
+
+        def load_weights(c):
+            passes = STREAM_PASSES[c]
+            first = FIRST_PASS[c]
             for r in range(4):
                 nc.sync.dma_start(
                     out=w_planes[r:P:32, first : first + passes, :].bitcast(I32),
@@ -121,15 +159,22 @@ def tile_blockrecurrentmodel_pa_kernel(
                     out=w_words[:, first + g0 : first + g1, :].bitcast(I32),
                     in_=stream_words[c][g0:g1].rearrange("g p n t -> p g (n t)").bitcast(I32),
                 )
-            for i in range(2):
-                load_w_piece()
 
+        rows_d = load_rows(D_STREAM)
         gb_raw = keep.tile([P, 6, 16], BF16)
         for c in range(3):
             nc.sync.dma_start(out=gb_raw[:, c, :PACK], in_=stream_gains[c].rearrange("(p t) -> p t", t=PACK))
             nc.sync.dma_start(out=gb_raw[:, 3 + c, :PACK], in_=stream_biases[c].rearrange("(p t) -> p t", t=PACK))
         gb_cols = keep.tile([P, 6, PACK], F32)
         nc.vector.tensor_copy(out=gb_cols[:], in_=gb_raw[:, :, :PACK])
+        rows_a = load_rows(A_STREAM)
+        load_weights(A_STREAM)
+        rows_s = load_rows(S_STREAM)
+        load_weights(S_STREAM)
+        load_weights(D_STREAM)
+        rows_sb = (rows_s, rows_a, rows_d)
+        for i in range(RAW_BUFS):
+            load_w_piece()
 
         gain_bc = keep.tile([P, DETER], BF16)
         nc.sync.dma_start(out=gain_bc[:], in_=ln_h_g.partition_broadcast(P))
@@ -142,80 +187,96 @@ def tile_blockrecurrentmodel_pa_kernel(
         nc.vector.memset(shift_cols[:], 0.0)
         nc.vector.memset(shift_cols[:, :, 4:5], 1.0)
 
-        def norm_factors(mean_var):
+        def inverse_std(mean_var):
             var_eps = small.tile([P, ROW_TILES], F32)
             nc.vector.tensor_scalar(out=var_eps[:], in0=mean_var[:, :, 1], scalar1=EPS, scalar2=None, op0=ALU.add)
             rstd = small.tile([P, ROW_TILES], F32)
             nc.gpsimd.tensor_tensor(out=rstd[:], in0=var_eps[:], in1=neg_half[:], op=ALU.pow)
+            return rstd
+
+        def minus_mean_over_std(mean_var, rstd):
             shift = small.tile([P, ROW_TILES], F32)
             nc.vector.scalar_tensor_tensor(
                 out=shift[:], in0=mean_var[:, :, 0], scalar=-1.0, in1=rstd[:], op0=ALU.mult, op1=ALU.mult
             )
-            return rstd, shift
+            return shift
 
-        for c in (2, 0, 1):
-            passes = STREAM_PASSES[c]
-            first = FIRST_PASS[c]
 
-            for pair in range(0, passes, 2):
-                count = min(2, passes - pair)
-                grouped = stage.tile([P, 2, ROWS, PACK], BF16, align_bytes=64)
-                for i in range(count):
-                    g = pair + i
-                    flipped = psum_t.tile([P, 2, ROWS], F32, tag="flipped")
-                    for u in range(2):
-                        for mt in range(ROW_TILES):
-                            nc.tensor.transpose(
-                                flipped[:, u, mt * P : (mt + 1) * P],
-                                rows_sb[c][:, mt, :].bitcast(F32)[:, 256 * g + u : 256 * (g + 1) : 2],
-                                ident[:],
-                            )
-                    copy_out = nc.vector.tensor_copy if i == 0 else nc.scalar.copy
-                    copy_out(out=grouped[:, i].bitcast(F32), in_=flipped[:].rearrange("p u r -> p r u"))
-                where = slice(first + pair, first + pair + count)
-                nc.vector.quantize_mx(
-                    out=act_codes[:, where, :].rearrange("p c r -> p (c r)").bitcast(FP8X4),
-                    scales=act_scales[:, where, :].rearrange("p c r -> p (c r)"),
-                    in_=grouped[:, :count].rearrange("p c r t -> p (c r t)"),
-                )
-
-            stats = small.tile([P, ROW_TILES, 6], F32)
-            mean_var = small.tile([P, ROW_TILES, 2], F32)
-            y = []
-            for mt in range(ROW_TILES):
-                y_mt = psum_acc.tile([P, HID], F32, tag="acc")
-                y.append(y_mt)
-                for i in range(passes):
-                    nc.tensor.matmul_mx(
-                        out=y_mt[:],
-                        lhsT=act_codes[:, first + i, mt * P : (mt + 1) * P].bitcast(FP8X4),
-                        lhsT_scale=act_scales[:, first + i, mt * P : (mt + 1) * P],
-                        rhs=w_words[:, first + i, :].bitcast(FP8X4),
-                        rhs_scale=w_planes[:, first + i, :],
-                        start=(i == 0),
-                        stop=(i == passes - 1),
-                    )
-                nc.vector.bn_stats(out=stats[:, mt, :], in_=y_mt[:])
-                nc.vector.bn_aggr(out=mean_var[:, mt, :], in_=stats[:, mt, :])
-            rstd, shift = norm_factors(mean_var)
-
-            z = []
-            for mt in range(ROW_TILES):
-                z_mt = normed.tile([P, PACK, P], F32, tag="z")
-                z.append(z_mt)
-                nc.scalar.activation(
-                    out=z_mt[:],
-                    in_=y[mt][:].rearrange("p (m t) -> p t m", t=PACK),
-                    func=ACT.Identity,
-                    scale=rstd[:, mt : mt + 1],
-                    bias=shift[:, mt : mt + 1],
-                )
-            x_planes = stage.tile([P, PACK, ROWS], BF16)
-            for half in range(2):
-                flipped = psum_t.tile([P, 2, ROWS], F32, tag="flipped")
+        def flip_rows(c, pair):
+            count = min(2, STREAM_PASSES[c] - pair)
+            grouped = stage.tile([P, 2, ROWS, PACK], BF16, align_bytes=64)
+            for i in range(count):
+                g = pair + i
+                flipped = psum.tile([P, 2, ROWS], F32, tag="bank")
                 for u in range(2):
                     for mt in range(ROW_TILES):
-                        nc.tensor.transpose(flipped[:, u, mt * P : (mt + 1) * P], z[mt][:, 2 * half + u, :], ident[:])
+                        nc.tensor.transpose(
+                            flipped[:, u, mt * P : (mt + 1) * P],
+                            rows_sb[c][:, mt, :].bitcast(F32)[:, 256 * g + u : 256 * (g + 1) : 2],
+                            ident[:],
+                        )
+                nc.scalar.copy(out=grouped[:, i].bitcast(F32), in_=flipped[:].rearrange("p u r -> p r u"))
+            return grouped
+
+        def quantise_rows(c, pair, grouped):
+            count = min(2, STREAM_PASSES[c] - pair)
+            where = slice(FIRST_PASS[c] + pair, FIRST_PASS[c] + pair + count)
+            nc.vector.quantize_mx(
+                out=act_codes[:, where, :].rearrange("p c r -> p (c r)").bitcast(FP8X4),
+                scales=act_scales[:, where, :].rearrange("p c r -> p (c r)"),
+                in_=grouped[:, :count].rearrange("p c r t -> p (c r t)"),
+            )
+
+        y = {}
+        stream_rstd = {}
+        stream_shift = {}
+        z = {}
+
+        def multiply_stream(c):
+            for mt in range(ROW_TILES):
+                y_mt = psum.tile([P, HID], F32, tag="bank")
+                y[(c, mt)] = y_mt
+                for i in range(STREAM_PASSES[c]):
+                    nc.tensor.matmul_mx(
+                        out=y_mt[:],
+                        lhsT=act_codes[:, FIRST_PASS[c] + i, mt * P : (mt + 1) * P].bitcast(FP8X4),
+                        lhsT_scale=act_scales[:, FIRST_PASS[c] + i, mt * P : (mt + 1) * P],
+                        rhs=w_words[:, FIRST_PASS[c] + i, :].bitcast(FP8X4),
+                        rhs_scale=w_planes[:, FIRST_PASS[c] + i, :],
+                        start=(i == 0),
+                        stop=(i == STREAM_PASSES[c] - 1),
+                    )
+
+        def stream_statistics(c):
+            stats = small.tile([P, ROW_TILES, 6], F32)
+            mean_var_c = small.tile([P, ROW_TILES, 2], F32)
+            for mt in range(ROW_TILES):
+                nc.vector.bn_stats(out=stats[:, mt, :], in_=y[(c, mt)][:])
+                nc.vector.bn_aggr(out=mean_var_c[:, mt, :], in_=stats[:, mt, :])
+            stream_rstd[c] = inverse_std(mean_var_c)
+            stream_shift[c] = minus_mean_over_std(mean_var_c, stream_rstd[c])
+
+        def normalise_stream(c):
+            for mt in range(ROW_TILES):
+                z_mt = normed.tile([P, PACK, P], F32, tag="z")
+                z[(c, mt)] = z_mt
+                nc.scalar.activation(
+                    out=z_mt[:],
+                    in_=y[(c, mt)][:].rearrange("p (m t) -> p t m", t=PACK),
+                    func=ACT.Identity,
+                    scale=stream_rstd[c][:, mt : mt + 1],
+                    bias=stream_shift[c][:, mt : mt + 1],
+                )
+
+        def flip_stream(c):
+            x_planes = stage.tile([P, PACK, ROWS], BF16)
+            for half in range(2):
+                flipped = psum.tile([P, 2, ROWS], F32, tag="bank")
+                for u in range(2):
+                    for mt in range(ROW_TILES):
+                        nc.tensor.transpose(
+                            flipped[:, u, mt * P : (mt + 1) * P], z[(c, mt)][:, 2 * half + u, :], ident[:]
+                        )
                 for u in range(2):
                     t = 2 * half + u
                     nc.scalar.activation(
@@ -225,6 +286,9 @@ def tile_blockrecurrentmodel_pa_kernel(
                         scale=gb_cols[:, c, t : t + 1],
                         bias=gb_cols[:, 3 + c, t : t + 1],
                     )
+            return x_planes
+
+        def quantise_stream(c, x_planes):
             x_grouped = stage.tile([P, ROWS, PACK], BF16, align_bytes=64)
             nc.vector.tensor_copy(out=x_grouped[:], in_=x_planes[:].rearrange("p t r -> p r t"))
             nc.vector.quantize_mx(
@@ -233,34 +297,44 @@ def tile_blockrecurrentmodel_pa_kernel(
                 in_=x_grouped[:].rearrange("p r t -> p (r t)"),
             )
 
-        for g in range(BLOCKS):
-            w_codes = []
-            w_scales = []
-            for c in range(BLOCK_PASSES):
-                if len(w_raw) == g * BLOCK_PASSES + c:
-                    load_w_piece()
-                raw = w_raw[g * BLOCK_PASSES + c]
-                w_grouped = w_grouped_pool.tile([P, HID, PACK], BF16, align_bytes=64)
-                nc.vector.tensor_copy(
-                    out=w_grouped[:, :VECTOR_COLS, :].rearrange("p (n i) j -> p n j i", i=4),
-                    in_=raw[:, :, :VECTOR_COLS].rearrange("p j (n i) -> p n j i", i=4),
-                )
-                nc.scalar.copy(
-                    out=w_grouped[:, VECTOR_COLS:, :].rearrange("p (n i) j -> p n j i", i=4),
-                    in_=raw[:, :, VECTOR_COLS:].rearrange("p j (n i) -> p n j i", i=4),
-                )
-                codes = w_packed_pool.tile([P, HID], U32, align_bytes=64)
-                scales = w_packed_pool.tile([P, HID], U8, align_bytes=64)
-                nc.vector.quantize_mx(
-                    out=codes[:].bitcast(FP8X4), scales=scales[:], in_=w_grouped[:].rearrange("p n j -> p (n j)")
-                )
-                w_codes.append(codes)
-                w_scales.append(scales)
+        waiting = None
+        for c in (D_STREAM, A_STREAM, S_STREAM):
+            for pair in range(0, STREAM_PASSES[c], 2):
+                grouped = flip_rows(c, pair)
+                if waiting is not None:
+                    quantise_rows(*waiting)
+                waiting = (c, pair, grouped)
+        quantise_rows(*waiting)
 
-            cols = slice(g * HID, (g + 1) * HID)
+        multiply_stream(A_STREAM)
+        stream_statistics(A_STREAM)
+        multiply_stream(S_STREAM)
+        stream_statistics(S_STREAM)
+        multiply_stream(D_STREAM)
+        normalise_stream(A_STREAM)
+        normalise_stream(S_STREAM)
+        advance_w()
+        a_planes = flip_stream(A_STREAM)
+        advance_w()
+        s_planes = flip_stream(S_STREAM)
+        stream_statistics(D_STREAM)
+        advance_w()
+        normalise_stream(D_STREAM)
+        quantise_stream(A_STREAM, a_planes)
+        quantise_stream(S_STREAM, s_planes)
+        advance_w()
+        d_planes = flip_stream(D_STREAM)
+        advance_w()
+        advance_w()
+        quantise_stream(D_STREAM, d_planes)
+
+        acc = {}
+
+        def multiply_block(g):
             for mt in range(ROW_TILES):
                 rows = slice(mt * P, (mt + 1) * P)
-                acc = psum_acc.tile([P, HID], F32, tag="acc")
+                acc_mt = psum.tile([P, HID], F32, tag="bank")
+                acc[(g, mt)] = acc_mt
                 for c in range(BLOCK_PASSES):
                     if c == 0:
                         lhs_codes = act_codes[:, FIRST_PASS[D_STREAM] + g, rows]
@@ -269,22 +343,39 @@ def tile_blockrecurrentmodel_pa_kernel(
                         lhs_codes = x_codes[:, c - 1, rows]
                         lhs_scales = x_scales[:, c - 1, rows]
                     nc.tensor.matmul_mx(
-                        out=acc[:],
+                        out=acc_mt[:],
                         lhsT=lhs_codes.bitcast(FP8X4),
                         lhsT_scale=lhs_scales,
-                        rhs=w_codes[c][:].bitcast(FP8X4),
-                        rhs_scale=w_scales[c][:],
+                        rhs=w_codes[g * BLOCK_PASSES + c][:].bitcast(FP8X4),
+                        rhs_scale=w_scales[g * BLOCK_PASSES + c][:],
                         start=(c == 0),
                         stop=(c == BLOCK_PASSES - 1),
                     )
-                nc.vector.bn_stats(out=h_stats[:, mt, g, :], in_=acc[:])
-                nc.vector.tensor_tensor(out=scaled[:, mt, cols], in0=acc[:], in1=gain_bc[:, cols], op=ALU.mult)
+
+        def block_statistics(g):
+            for mt in range(ROW_TILES):
+                nc.vector.bn_stats(out=h_stats[:, mt, g, :], in_=acc[(g, mt)][:])
+
+        def scale_block(g):
+            cols = slice(g * HID, (g + 1) * HID)
+            for mt in range(ROW_TILES):
+                nc.vector.tensor_tensor(out=scaled[:, mt, cols], in0=acc[(g, mt)][:], in1=gain_bc[:, cols], op=ALU.mult)
+
+        for g in range(BLOCKS):
+            while len(w_codes) < (g + 1) * BLOCK_PASSES:
+                advance_w()
+            multiply_block(g)
+            if g > 0:
+                block_statistics(g - 1)
+                scale_block(g - 1)
+        block_statistics(BLOCKS - 1)
 
         h_mean_var = small.tile([P, ROW_TILES, 2], F32)
         for mt in range(ROW_TILES):
             nc.vector.bn_aggr(out=h_mean_var[:, mt, :], in_=h_stats[:, mt].rearrange("p g s -> p (g s)"))
-        h_rstd, h_shift = norm_factors(h_mean_var)
-
+        h_rstd = inverse_std(h_mean_var)
+        scale_block(BLOCKS - 1)
+        h_shift = minus_mean_over_std(h_mean_var, h_rstd)
         rest = h_shift
         for part in range(3):
             nc.vector.tensor_copy(out=shift_cols[:, :, part], in_=rest[:])
@@ -292,7 +383,7 @@ def tile_blockrecurrentmodel_pa_kernel(
                 smaller = small.tile([P, ROW_TILES], F32, tag="rest")
                 nc.vector.tensor_tensor(out=smaller[:], in0=rest[:], in1=shift_cols[:, :, part], op=ALU.subtract)
                 rest = smaller
-        shift_flipped = psum_t.tile([P, ROW_TILES, P], BF16, tag="flipped")
+        shift_flipped = psum.tile([P, ROW_TILES, P], BF16, tag="bank")
         for mt in range(ROW_TILES):
             nc.tensor.transpose(shift_flipped[:, mt, :], shift_cols[:, mt, :], ident_bf[:])
         shift_rows = keep.tile([P, ROW_TILES, P], BF16)
@@ -301,18 +392,13 @@ def tile_blockrecurrentmodel_pa_kernel(
         for mt in range(ROW_TILES):
             for g in range(BLOCKS):
                 cols = slice(g * HID, (g + 1) * HID)
-                offset = psum_acc.tile([P, HID], F32, tag="acc")
+                offset = psum.tile([P, HID], F32, tag="bank")
                 nc.tensor.matmul(
                     out=offset[:], lhsT=shift_rows[:, mt, :], rhs=gain_bias_rows[:, cols], start=True, stop=True
                 )
                 v = scaled[:, mt, cols]
                 nc.vector.scalar_tensor_tensor(
-                    out=v,
-                    in0=v,
-                    scalar=h_rstd[:, mt : mt + 1],
-                    in1=offset[:],
-                    op0=ALU.mult,
-                    op1=ALU.add,
+                    out=v, in0=v, scalar=h_rstd[:, mt : mt + 1], in1=offset[:], op0=ALU.mult, op1=ALU.add
                 )
                 nc.scalar.activation(out=v, in_=v, func=ACT.Silu)
                 nc.sync.dma_start(out=out[mt * P : (mt + 1) * P, cols], in_=v)

@@ -30,6 +30,7 @@ EPS = 1e-3
 LOAD_COLS = 1024
 RAW_BUFS = 7
 PACKED_BUFS = 12
+EARLY_PIECES = 6
 QUANTISE_LAG = 2
 
 FLOPS = 2 * ROWS * ((1024 + 512 + 4096) * HID + BLOCK_PASSES * K_PASS * DETER)
@@ -106,7 +107,7 @@ def tile_blockrecurrentmodel_pa_kernel(
 
         def regroup_w_piece():
             i = len(w_grouped)
-            by_vector = i % 8 in (0, 3, 6)
+            by_vector = i % 3 != 1 if i < EARLY_PIECES else i % 16 in (0, 3, 6, 9, 12)
             grouped = w_grouped_pool.tile(
                 [P, HID, PACK], BF16, align_bytes=64, tag="by_vector" if by_vector else "by_scalar"
             )
@@ -163,8 +164,8 @@ def tile_blockrecurrentmodel_pa_kernel(
         rows_d = load_rows(D_STREAM)
         gb_raw = keep.tile([P, 6, 16], BF16)
         for c in range(3):
-            nc.sync.dma_start(out=gb_raw[:, c, :PACK], in_=stream_gains[c].rearrange("(p t) -> p t", t=PACK))
-            nc.sync.dma_start(out=gb_raw[:, 3 + c, :PACK], in_=stream_biases[c].rearrange("(p t) -> p t", t=PACK))
+            nc.gpsimd.dma_start(out=gb_raw[:, c, :PACK], in_=stream_gains[c].rearrange("(p t) -> p t", t=PACK))
+            nc.gpsimd.dma_start(out=gb_raw[:, 3 + c, :PACK], in_=stream_biases[c].rearrange("(p t) -> p t", t=PACK))
         gb_cols = keep.tile([P, 6, PACK], F32)
         nc.vector.tensor_copy(out=gb_cols[:], in_=gb_raw[:, :, :PACK])
         rows_a = load_rows(A_STREAM)
@@ -181,8 +182,8 @@ def tile_blockrecurrentmodel_pa_kernel(
 
         gain_bias_rows = keep.tile([P, DETER], BF16)
         nc.gpsimd.memset(gain_bias_rows[:].bitcast(F32), 0.0)
-        nc.sync.dma_start(out=gain_bias_rows[0:4, :], in_=ln_h_g.partition_broadcast(4))
-        nc.sync.dma_start(out=gain_bias_rows[4:5, :], in_=ln_h_b.partition_broadcast(1))
+        nc.gpsimd.dma_start(out=gain_bias_rows[0:4, :], in_=ln_h_g.partition_broadcast(4))
+        nc.gpsimd.dma_start(out=gain_bias_rows[4:5, :], in_=ln_h_b.partition_broadcast(1))
         shift_cols = keep.tile([P, ROW_TILES, P], BF16)
         nc.vector.memset(shift_cols[:], 0.0)
         nc.vector.memset(shift_cols[:, :, 4:5], 1.0)
@@ -236,9 +237,10 @@ def tile_blockrecurrentmodel_pa_kernel(
             for mt in range(ROW_TILES):
                 y_mt = psum.tile([P, HID], F32, tag="bank")
                 y[(c, mt)] = y_mt
-                for i in range(STREAM_PASSES[c]):
+            for i in range(STREAM_PASSES[c]):
+                for mt in range(ROW_TILES):
                     nc.tensor.matmul_mx(
-                        out=y_mt[:],
+                        out=y[(c, mt)][:],
                         lhsT=act_codes[:, FIRST_PASS[c] + i, mt * P : (mt + 1) * P].bitcast(FP8X4),
                         lhsT_scale=act_scales[:, FIRST_PASS[c] + i, mt * P : (mt + 1) * P],
                         rhs=w_words[:, FIRST_PASS[c] + i, :].bitcast(FP8X4),
@@ -365,16 +367,17 @@ def tile_blockrecurrentmodel_pa_kernel(
             while len(w_codes) < (g + 1) * BLOCK_PASSES:
                 advance_w()
             multiply_block(g)
-            if g > 0:
+            if g >= 1:
                 block_statistics(g - 1)
-                scale_block(g - 1)
+            if g >= 2:
+                scale_block(g - 2)
         block_statistics(BLOCKS - 1)
 
         h_mean_var = small.tile([P, ROW_TILES, 2], F32)
         for mt in range(ROW_TILES):
             nc.vector.bn_aggr(out=h_mean_var[:, mt, :], in_=h_stats[:, mt].rearrange("p g s -> p (g s)"))
         h_rstd = inverse_std(h_mean_var)
-        scale_block(BLOCKS - 1)
+        scale_block(BLOCKS - 2)
         h_shift = minus_mean_over_std(h_mean_var, h_rstd)
         rest = h_shift
         for part in range(3):
@@ -388,6 +391,7 @@ def tile_blockrecurrentmodel_pa_kernel(
             nc.tensor.transpose(shift_flipped[:, mt, :], shift_cols[:, mt, :], ident_bf[:])
         shift_rows = keep.tile([P, ROW_TILES, P], BF16)
         nc.scalar.copy(out=shift_rows[:], in_=shift_flipped[:])
+        scale_block(BLOCKS - 1)
 
         for mt in range(ROW_TILES):
             for g in range(BLOCKS):

@@ -81,6 +81,9 @@ def tile_blockrecurrentmodel_pa_kernel(
         make_identity(nc, ident_bf[:])
         neg_half = keep.tile([P, ROW_TILES], F32)
         nc.vector.memset(neg_half[:], -0.5)
+        first_silu = keep.tile([P, 1], F32)
+        nc.vector.memset(first_silu[:], 0.0)
+        nc.scalar.activation(out=first_silu[:], in_=first_silu[:], func=ACT.Silu)
 
         w_words = keep.tile([P, ALL_PASSES, HID * PACK], U8, align_bytes=64)
         w_planes = keep.tile([P, ALL_PASSES, HID], U8, align_bytes=64)
@@ -149,17 +152,18 @@ def tile_blockrecurrentmodel_pa_kernel(
         def load_weights(c):
             passes = STREAM_PASSES[c]
             first = FIRST_PASS[c]
-            for r in range(4):
-                nc.sync.dma_start(
-                    out=w_planes[r:P:32, first : first + passes, :].bitcast(I32),
-                    in_=stream_scales[c].rearrange("g (q r) n -> r q g n", r=4)[r].bitcast(I32),
-                )
             for g0 in range(0, passes, 4):
                 g1 = min(g0 + 4, passes)
                 nc.sync.dma_start(
                     out=w_words[:, first + g0 : first + g1, :].bitcast(I32),
                     in_=stream_words[c][g0:g1].rearrange("g p n t -> p g (n t)").bitcast(I32),
                 )
+                if g0 == 0:
+                    for r in range(4):
+                        nc.sync.dma_start(
+                            out=w_planes[r:P:32, first : first + passes, :].bitcast(I32),
+                            in_=stream_scales[c].rearrange("g (q r) n -> r q g n", r=4)[r].bitcast(I32),
+                        )
 
         rows_d = load_rows(D_STREAM)
         gb_raw = keep.tile([P, 6, 16], BF16)

@@ -116,8 +116,8 @@ def tile_blockrecurrentmodel_pa_kernel(
             )
             regroup = nc.vector.tensor_copy if by_vector else nc.scalar.copy
             regroup(
-                out=grouped[:].rearrange("p (n i) j -> p n j i", i=4),
-                in_=w_raw[i][:].rearrange("p j (n i) -> p n j i", i=4),
+                out=grouped[:].rearrange("p (n i) j -> p n j i", i=2),
+                in_=w_raw[i][:].rearrange("p j (n i) -> p n j i", i=2),
             )
             w_grouped.append(grouped)
             if len(w_raw) < PIECES:

from contextlib import ExitStack

import concourse.mybir as mybir
from concourse.masks import make_identity

FP8X4 = mybir.dt.float8_e4m3fn_x4
BF16 = mybir.dt.bfloat16
F32 = mybir.dt.float32
I32 = mybir.dt.int32
U32 = mybir.dt.uint32
U8 = mybir.dt.uint8
ALU = mybir.AluOpType
ACT = mybir.ActivationFunctionType

P = 128
PACK = 4
K_PASS = P * PACK
ROWS = 256
ROW_TILES = ROWS // P
HID = 512
BLOCKS = 8
DETER = BLOCKS * HID
S_STREAM, A_STREAM, D_STREAM = 0, 1, 2
STREAM_PASSES = (2, 1, 8)
FIRST_PASS = (0, 2, 3)
ALL_PASSES = 11
BLOCK_PASSES = 4
PIECES = BLOCKS * BLOCK_PASSES
EPS = 1e-3
LOAD_COLS = 1024
RAW_BUFS = 7
PACKED_BUFS = 12
EARLY_PIECES = 6
QUANTISE_LAG = 2

FLOPS = 2 * ROWS * ((1024 + 512 + 4096) * HID + BLOCK_PASSES * K_PASS * DETER)


def tile_blockrecurrentmodel_pa_kernel(
    tc,
    s,
    a,
    d,
    W_s_words,
    W_s_scales,
    W_a_words,
    W_a_scales,
    W_d_words,
    W_d_scales,
    ln_s_g,
    ln_s_b,
    ln_a_g,
    ln_a_b,
    ln_d_g,
    ln_d_b,
    W_hid,
    ln_h_g,
    ln_h_b,
    out,
):
    nc = tc.nc
    stream_rows = (s.flatten_outer_dims(), a.flatten_outer_dims(), d.flatten_outer_dims())
    stream_words = (W_s_words, W_a_words, W_d_words)
    stream_scales = (W_s_scales, W_a_scales, W_d_scales)
    stream_gains = (ln_s_g, ln_a_g, ln_d_g)
    stream_biases = (ln_s_b, ln_a_b, ln_d_b)

    with ExitStack() as pools:
        keep = pools.enter_context(tc.tile_pool(name="keep", bufs=1))
        small = pools.enter_context(tc.tile_pool(name="small", bufs=4))
        stage = pools.enter_context(tc.tile_pool(name="stage", bufs=2))
        normed = pools.enter_context(tc.tile_pool(name="normed", bufs=6))
        w_raw_pool = pools.enter_context(tc.tile_pool(name="w_raw", bufs=RAW_BUFS))
        w_grouped_pool = pools.enter_context(tc.tile_pool(name="w_grouped", bufs=3))
        w_packed_pool = pools.enter_context(tc.tile_pool(name="w_packed", bufs=PACKED_BUFS))
        psum = pools.enter_context(tc.psum_pool(name="psum", bufs=8))

        ident = keep.tile([P, P], F32)
        make_identity(nc, ident[:])
        ident_bf = keep.tile([P, P], BF16)
        make_identity(nc, ident_bf[:])
        neg_half = keep.tile([P, ROW_TILES], F32)
        nc.vector.memset(neg_half[:], -0.5)
        first_silu = keep.tile([P, 1], F32)
        nc.vector.memset(first_silu[:], 0.0)
        nc.scalar.activation(out=first_silu[:], in_=first_silu[:], func=ACT.Silu)

        w_words = keep.tile([P, ALL_PASSES, HID * PACK], U8, align_bytes=64)
        w_planes = keep.tile([P, ALL_PASSES, HID], U8, align_bytes=64)
        nc.vector.memset(w_planes[:].rearrange("p c n -> p (c n)").bitcast(I32), 0)
        act_codes = keep.tile([P, ALL_PASSES, ROWS], U32, align_bytes=64)
        act_scales = keep.tile([P, ALL_PASSES, ROWS], U8, align_bytes=64)
        x_codes = keep.tile([P, 3, ROWS], U32, align_bytes=64)
        x_scales = keep.tile([P, 3, ROWS], U8, align_bytes=64)
        scaled = keep.tile([P, ROW_TILES, DETER], F32)
        h_stats = keep.tile([P, ROW_TILES, BLOCKS, 6], F32)

        w_raw = []
        w_grouped = []
        w_codes = []
        w_scales = []

        def load_w_piece():
            g, c = divmod(len(w_raw), BLOCK_PASSES)
            raw = w_raw_pool.tile([P, PACK, HID], BF16)
            nc.sync.dma_start(
                out=raw[:], in_=W_hid[g, c * K_PASS : (c + 1) * K_PASS, :].rearrange("(p j) n -> p j n", j=PACK)
            )
            w_raw.append(raw)

        def regroup_w_piece():
            i = len(w_grouped)
            by_vector = i % 3 != 1 if i < EARLY_PIECES else i % 16 in (0, 3, 6, 9, 12)
            grouped = w_grouped_pool.tile(
                [P, HID, PACK], BF16, align_bytes=64, tag="by_vector" if by_vector else "by_scalar"
            )
            regroup = nc.vector.tensor_copy if by_vector else nc.scalar.copy
            regroup(
                out=grouped[:].rearrange("p (n i) j -> p n j i", i=2),
                in_=w_raw[i][:].rearrange("p j (n i) -> p n j i", i=2),
            )
            w_grouped.append(grouped)
            if len(w_raw) < PIECES:
                load_w_piece()

        def quantise_w_piece():
            i = len(w_codes)
            codes = w_packed_pool.tile([P, HID], U32, align_bytes=64)
            scales = w_packed_pool.tile([P, HID], U8, align_bytes=64)
            nc.vector.quantize_mx(
                out=codes[:].bitcast(FP8X4), scales=scales[:], in_=w_grouped[i][:].rearrange("p n j -> p (n j)")
            )
            w_codes.append(codes)
            w_scales.append(scales)

        def advance_w():
            if len(w_grouped) < PIECES:
                regroup_w_piece()
            if len(w_grouped) - len(w_codes) > QUANTISE_LAG or len(w_grouped) == PIECES:
                quantise_w_piece()

        def load_rows(c):
            width = STREAM_PASSES[c] * K_PASS
            rows_c = keep.tile([P, ROW_TILES, width], BF16, name="rows_%d" % c)
            for k0 in range(0, width, LOAD_COLS):
                k1 = min(k0 + LOAD_COLS, width)
                nc.sync.dma_start(
                    out=rows_c[:, :, k0:k1], in_=stream_rows[c].rearrange("(m p) k -> p m k", p=P)[:, :, k0:k1]
                )
            return rows_c

        def load_weights(c):
            passes = STREAM_PASSES[c]
            first = FIRST_PASS[c]
            for g0 in range(0, passes, 4):
                g1 = min(g0 + 4, passes)
                nc.sync.dma_start(
                    out=w_words[:, first + g0 : first + g1, :].bitcast(I32),
                    in_=stream_words[c][g0:g1].rearrange("g p n t -> p g (n t)").bitcast(I32),
                )
                if g0 == 0:
                    for r in range(4):
                        nc.sync.dma_start(
                            out=w_planes[r:P:32, first : first + passes, :].bitcast(I32),
                            in_=stream_scales[c].rearrange("g (q r) n -> r q g n", r=4)[r].bitcast(I32),
                        )

        rows_d = load_rows(D_STREAM)
        gb_raw = keep.tile([P, 6, 16], BF16)
        for c in range(3):
            nc.gpsimd.dma_start(out=gb_raw[:, c, :PACK], in_=stream_gains[c].rearrange("(p t) -> p t", t=PACK))
            nc.gpsimd.dma_start(out=gb_raw[:, 3 + c, :PACK], in_=stream_biases[c].rearrange("(p t) -> p t", t=PACK))
        gb_cols = keep.tile([P, 6, PACK], F32)
        nc.vector.tensor_copy(out=gb_cols[:], in_=gb_raw[:, :, :PACK])
        rows_a = load_rows(A_STREAM)
        load_weights(A_STREAM)
        rows_s = load_rows(S_STREAM)
        load_weights(S_STREAM)
        load_weights(D_STREAM)
        rows_sb = (rows_s, rows_a, rows_d)
        for i in range(RAW_BUFS):
            load_w_piece()

        gain_bc = keep.tile([P, DETER], BF16)
        nc.sync.dma_start(out=gain_bc[:], in_=ln_h_g.partition_broadcast(P))

        gain_bias_rows = keep.tile([P, DETER], BF16)
        nc.gpsimd.memset(gain_bias_rows[:].bitcast(F32), 0.0)
        nc.gpsimd.dma_start(out=gain_bias_rows[0:4, :], in_=ln_h_g.partition_broadcast(4))
        nc.gpsimd.dma_start(out=gain_bias_rows[4:5, :], in_=ln_h_b.partition_broadcast(1))
        shift_cols = keep.tile([P, ROW_TILES, P], BF16)
        nc.vector.memset(shift_cols[:], 0.0)
        nc.vector.memset(shift_cols[:, :, 4:5], 1.0)

        def inverse_std(mean_var):
            var_eps = small.tile([P, ROW_TILES], F32)
            nc.vector.tensor_scalar(out=var_eps[:], in0=mean_var[:, :, 1], scalar1=EPS, scalar2=None, op0=ALU.add)
            rstd = small.tile([P, ROW_TILES], F32)
            nc.gpsimd.tensor_tensor(out=rstd[:], in0=var_eps[:], in1=neg_half[:], op=ALU.pow)
            return rstd

        def minus_mean_over_std(mean_var, rstd):
            shift = small.tile([P, ROW_TILES], F32)
            nc.vector.scalar_tensor_tensor(
                out=shift[:], in0=mean_var[:, :, 0], scalar=-1.0, in1=rstd[:], op0=ALU.mult, op1=ALU.mult
            )
            return shift


        def flip_rows(c, pair):
            count = min(2, STREAM_PASSES[c] - pair)
            grouped = stage.tile([P, 2, ROWS, PACK], BF16, align_bytes=64)
            for i in range(count):
                g = pair + i
                flipped = psum.tile([P, 2, ROWS], F32, tag="bank")
                for u in range(2):
                    for mt in range(ROW_TILES):
                        nc.tensor.transpose(
                            flipped[:, u, mt * P : (mt + 1) * P],
                            rows_sb[c][:, mt, :].bitcast(F32)[:, 256 * g + u : 256 * (g + 1) : 2],
                            ident[:],
                        )
                nc.scalar.copy(out=grouped[:, i].bitcast(F32), in_=flipped[:].rearrange("p u r -> p r u"))
            return grouped

        def quantise_rows(c, pair, grouped):
            count = min(2, STREAM_PASSES[c] - pair)
            where = slice(FIRST_PASS[c] + pair, FIRST_PASS[c] + pair + count)
            nc.vector.quantize_mx(
                out=act_codes[:, where, :].rearrange("p c r -> p (c r)").bitcast(FP8X4),
                scales=act_scales[:, where, :].rearrange("p c r -> p (c r)"),
                in_=grouped[:, :count].rearrange("p c r t -> p (c r t)"),
            )

        y = {}
        stream_rstd = {}
        stream_shift = {}
        z = {}

        def multiply_stream(c):
            for mt in range(ROW_TILES):
                y_mt = psum.tile([P, HID], F32, tag="bank")
                y[(c, mt)] = y_mt
            for i in range(STREAM_PASSES[c]):
                for mt in range(ROW_TILES):
                    nc.tensor.matmul_mx(
                        out=y[(c, mt)][:],
                        lhsT=act_codes[:, FIRST_PASS[c] + i, mt * P : (mt + 1) * P].bitcast(FP8X4),
                        lhsT_scale=act_scales[:, FIRST_PASS[c] + i, mt * P : (mt + 1) * P],
                        rhs=w_words[:, FIRST_PASS[c] + i, :].bitcast(FP8X4),
                        rhs_scale=w_planes[:, FIRST_PASS[c] + i, :],
                        start=(i == 0),
                        stop=(i == STREAM_PASSES[c] - 1),
                    )

        def stream_statistics(c):
            stats = small.tile([P, ROW_TILES, 6], F32)
            mean_var_c = small.tile([P, ROW_TILES, 2], F32)
            for mt in range(ROW_TILES):
                nc.vector.bn_stats(out=stats[:, mt, :], in_=y[(c, mt)][:])
                nc.vector.bn_aggr(out=mean_var_c[:, mt, :], in_=stats[:, mt, :])
            stream_rstd[c] = inverse_std(mean_var_c)
            stream_shift[c] = minus_mean_over_std(mean_var_c, stream_rstd[c])

        def normalise_stream(c):
            for mt in range(ROW_TILES):
                z_mt = normed.tile([P, PACK, P], F32, tag="z")
                z[(c, mt)] = z_mt
                nc.scalar.activation(
                    out=z_mt[:],
                    in_=y[(c, mt)][:].rearrange("p (m t) -> p t m", t=PACK),
                    func=ACT.Identity,
                    scale=stream_rstd[c][:, mt : mt + 1],
                    bias=stream_shift[c][:, mt : mt + 1],
                )

        def flip_stream(c):
            x_planes = stage.tile([P, PACK, ROWS], BF16)
            for half in range(2):
                flipped = psum.tile([P, 2, ROWS], F32, tag="bank")
                for u in range(2):
                    for mt in range(ROW_TILES):
                        nc.tensor.transpose(
                            flipped[:, u, mt * P : (mt + 1) * P], z[(c, mt)][:, 2 * half + u, :], ident[:]
                        )
                for u in range(2):
                    t = 2 * half + u
                    nc.scalar.activation(
                        out=x_planes[:, t, :],
                        in_=flipped[:, u, :],
                        func=ACT.Silu,
                        scale=gb_cols[:, c, t : t + 1],
                        bias=gb_cols[:, 3 + c, t : t + 1],
                    )
            return x_planes

        def quantise_stream(c, x_planes):
            x_grouped = stage.tile([P, ROWS, PACK], BF16, align_bytes=64)
            nc.vector.tensor_copy(out=x_grouped[:], in_=x_planes[:].rearrange("p t r -> p r t"))
            nc.vector.quantize_mx(
                out=x_codes[:, c, :].bitcast(FP8X4),
                scales=x_scales[:, c, :],
                in_=x_grouped[:].rearrange("p r t -> p (r t)"),
            )

        waiting = None
        for c in (D_STREAM, A_STREAM, S_STREAM):
            for pair in range(0, STREAM_PASSES[c], 2):
                grouped = flip_rows(c, pair)
                if waiting is not None:
                    quantise_rows(*waiting)
                waiting = (c, pair, grouped)
        quantise_rows(*waiting)

        multiply_stream(A_STREAM)
        stream_statistics(A_STREAM)
        multiply_stream(S_STREAM)
        stream_statistics(S_STREAM)
        multiply_stream(D_STREAM)
        normalise_stream(A_STREAM)
        normalise_stream(S_STREAM)
        advance_w()
        a_planes = flip_stream(A_STREAM)
        advance_w()
        s_planes = flip_stream(S_STREAM)
        stream_statistics(D_STREAM)
        advance_w()
        normalise_stream(D_STREAM)
        quantise_stream(A_STREAM, a_planes)
        quantise_stream(S_STREAM, s_planes)
        advance_w()
        d_planes = flip_stream(D_STREAM)
        advance_w()
        advance_w()
        quantise_stream(D_STREAM, d_planes)

        acc = {}

        def multiply_block(g):
            for mt in range(ROW_TILES):
                rows = slice(mt * P, (mt + 1) * P)
                acc_mt = psum.tile([P, HID], F32, tag="bank")
                acc[(g, mt)] = acc_mt
                for c in range(BLOCK_PASSES):
                    if c == 0:
                        lhs_codes = act_codes[:, FIRST_PASS[D_STREAM] + g, rows]
                        lhs_scales = act_scales[:, FIRST_PASS[D_STREAM] + g, rows]
                    else:
                        lhs_codes = x_codes[:, c - 1, rows]
                        lhs_scales = x_scales[:, c - 1, rows]
                    nc.tensor.matmul_mx(
                        out=acc_mt[:],
                        lhsT=lhs_codes.bitcast(FP8X4),
                        lhsT_scale=lhs_scales,
                        rhs=w_codes[g * BLOCK_PASSES + c][:].bitcast(FP8X4),
                        rhs_scale=w_scales[g * BLOCK_PASSES + c][:],
                        start=(c == 0),
                        stop=(c == BLOCK_PASSES - 1),
                    )

        def block_statistics(g):
            for mt in range(ROW_TILES):
                nc.vector.bn_stats(out=h_stats[:, mt, g, :], in_=acc[(g, mt)][:])

        def scale_block(g):
            cols = slice(g * HID, (g + 1) * HID)
            for mt in range(ROW_TILES):
                nc.vector.tensor_tensor(out=scaled[:, mt, cols], in0=acc[(g, mt)][:], in1=gain_bc[:, cols], op=ALU.mult)

        for g in range(BLOCKS):
            while len(w_codes) < (g + 1) * BLOCK_PASSES:
                advance_w()
            multiply_block(g)
            if g >= 1:
                block_statistics(g - 1)
            if g >= 2:
                scale_block(g - 2)
        block_statistics(BLOCKS - 1)

        h_mean_var = small.tile([P, ROW_TILES, 2], F32)
        for mt in range(ROW_TILES):
            nc.vector.bn_aggr(out=h_mean_var[:, mt, :], in_=h_stats[:, mt].rearrange("p g s -> p (g s)"))
        h_rstd = inverse_std(h_mean_var)
        scale_block(BLOCKS - 2)
        h_shift = minus_mean_over_std(h_mean_var, h_rstd)
        rest = h_shift
        for part in range(3):
            nc.vector.tensor_copy(out=shift_cols[:, :, part], in_=rest[:])
            if part < 2:
                smaller = small.tile([P, ROW_TILES], F32, tag="rest")
                nc.vector.tensor_tensor(out=smaller[:], in0=rest[:], in1=shift_cols[:, :, part], op=ALU.subtract)
                rest = smaller
        shift_flipped = psum.tile([P, ROW_TILES, P], BF16, tag="bank")
        for mt in range(ROW_TILES):
            nc.tensor.transpose(shift_flipped[:, mt, :], shift_cols[:, mt, :], ident_bf[:])
        shift_rows = keep.tile([P, ROW_TILES, P], BF16)
        nc.scalar.copy(out=shift_rows[:], in_=shift_flipped[:])
        scale_block(BLOCKS - 1)

        for mt in range(ROW_TILES):
            for g in range(BLOCKS):
                cols = slice(g * HID, (g + 1) * HID)
                offset = psum.tile([P, HID], F32, tag="bank")
                nc.tensor.matmul(
                    out=offset[:], lhsT=shift_rows[:, mt, :], rhs=gain_bias_rows[:, cols], start=True, stop=True
                )
                v = scaled[:, mt, cols]
                nc.vector.scalar_tensor_tensor(
                    out=v, in0=v, scalar=h_rstd[:, mt : mt + 1], in1=offset[:], op0=ALU.mult, op1=ALU.add
                )
                nc.scalar.activation(out=v, in_=v, func=ACT.Silu)
                nc.sync.dma_start(out=out[mt * P : (mt + 1) * P, cols], in_=v)
